import numpy as np
import ml_dtypes


def mxq(x, axis, fmt="e4m3"):
    dtype, down = {"e4m3": (ml_dtypes.float8_e4m3fn, 7), "e5m2": (ml_dtypes.float8_e5m2, 14)}[fmt]
    v = np.moveaxis(np.asarray(x, np.float32).astype(ml_dtypes.bfloat16).astype(np.float64), axis, -1)
    blocks = v.reshape(v.shape[:-1] + (-1, 32))
    amax = np.abs(blocks).max(-1, keepdims=True)
    byte = np.maximum(np.where(amax > 0, np.frexp(amax)[1] - 1 + 127, 0) - down, 1)
    scale = np.exp2(byte - 127.0)
    codes = (blocks / scale).astype(np.float32).astype(dtype).astype(np.float64)
    return np.moveaxis((codes * scale).reshape(v.shape), -1, axis)


WIDE = False


def mx_kscale(k):
    if not WIDE:
        return np.ones(k)
    levels = np.array([10, -10, 5, -5, 0])
    if k % 512:
        return np.exp2(np.random.permutation(np.resize(levels, k // 32))).repeat(32)
    a = np.empty((k // 512, 16))
    for p in range(k // 512):
        a[p, :8] = np.random.permutation(np.resize(levels, 8))
        for g in range(8):
            far = levels[np.abs(levels - a[p, g]) >= 10]
            a[p, g + 8] = far[np.random.randint(len(far))]
    return np.exp2(a.ravel()).repeat(32)


BF16 = ml_dtypes.bfloat16


def bf(x):
    return np.asarray(x, np.float32).astype(BF16)


def f64(x):
    return np.asarray(x).astype(np.float64)


L, T, F, D = 4, 128, 1536, 512


def setup_inputs():
    s, t = mx_kscale(D), mx_kscale(F)
    return {"x": bf(np.random.standard_normal((L, T, D)) * s),
            "W_enc": bf(np.random.standard_normal((L, F, D)) / np.sqrt(D) / s * t[:, None]),
            "b_enc": bf(np.random.standard_normal((L, F)) * 0.2 * t),
            "b_dec": bf(np.random.standard_normal((L, D)) * 0.3),
            "W_dec": bf(np.random.standard_normal((L, L, F, D)) / np.sqrt(F) / t[:, None]),
            "dec_mask": np.triu(np.ones((L, L), dtype=bool))}


def reference(x, W_enc, b_enc, b_dec, W_dec, dec_mask):
    pre = mxq(f64(x), 2, "e4m3") @ mxq(f64(W_enc), 2, "e4m3").transpose(0, 2, 1)
    acts = np.maximum(pre + f64(b_enc)[:, None, :], 0.0)
    aq = mxq(acts, 2, "e4m3")
    Wd = f64(W_dec)
    keep = np.asarray(dec_mask)
    recon = []
    for j in range(L):
        src = np.nonzero(keep[:, j])[0]
        a = np.concatenate([aq[i] for i in src], axis=1)
        w = mxq(Wd[src, j], 1, "e4m3").reshape(len(src) * F, D)
        recon.append((a @ w) + f64(b_dec)[j])
    return np.stack(recon)

@@ -1,0 +1,275 @@
+from contextlib import ExitStack
+
+import concourse.mybir as mybir
+from concourse.masks import make_identity
+
+F32 = mybir.dt.float32
+BF16 = mybir.dt.bfloat16
+U32 = mybir.dt.uint32
+U8 = mybir.dt.uint8
+FP8X4 = mybir.dt.float8_e4m3fn_x4
+ADD = mybir.AluOpType.add
+
+L, T, F, D = 4, 128, 1536, 512
+P = 128
+PACK = 4
+KP = P * PACK
+G = F // KP
+BANK_DT = F32
+
+FLOPS = 2 * L * T * F * D + 2 * 10 * T * F * D
+BYTES = 2 * (L * T * D + L * F * D + L * F + L * D + 10 * F * D) + 4 * L * T * D
+
+LOOKAHEAD = 3
+BDEC_GROUP = 6
+FIRST_EPILOGUE_ROUND = 8
+S_COLS = [[192, 0], [448, 0], [512, 0], [512, 0], [512, 0], [512, 144], [512, 0], [512, 0], [512, 224], [512, 96], [512, 0], [512, 144], [512, 0], [512, 256], [512, 144]]
+
+
+def tile_crosslayertranscoder_kernel(tc, x, W_enc, b_enc, b_dec, W_dec, dec_mask, out):
+    nc = tc.nc
+    enc_chunks = [None] + [(l, g) for l in range(L) for g in range(G)]
+    dec_chunks = [(i, j, g) for i in range(L) for j in range(i, L) for g in range(G)]
+    n_enc = len(enc_chunks)
+    n_pairs = len(dec_chunks) // 2
+
+    with ExitStack() as ctx:
+        const = ctx.enter_context(tc.tile_pool(name="const", bufs=1))
+        rawp = ctx.enter_context(tc.tile_pool(name="rawp", bufs=3 * (LOOKAHEAD + 1)))
+        wgp = ctx.enter_context(tc.tile_pool(name="wgp", bufs=2))
+        wcp = ctx.enter_context(tc.tile_pool(name="wcp", bufs=2))
+        dgp = ctx.enter_context(tc.tile_pool(name="dgp", bufs=3))
+        dcp = ctx.enter_context(tc.tile_pool(name="dcp", bufs=5))
+        actp = ctx.enter_context(tc.tile_pool(name="actp", bufs=2))
+        otp = ctx.enter_context(tc.tile_pool(name="otp", bufs=2))
+        tpp = ctx.enter_context(tc.psum_pool(name="tpp", bufs=2))
+        epp = ctx.enter_context(tc.psum_pool(name="epp", bufs=2))
+        accp = ctx.enter_context(tc.psum_pool(name="accp", bufs=1))
+        ctx.enter_context(tc.manual_schedule())
+
+        ident = const.tile([P, P], F32, name="ident")
+        make_identity(nc, ident[:])
+        benc = const.tile([P, L * G, PACK], BF16, name="benc")
+        nc.scalar.dma_start(
+            out=benc[:], in_=b_enc.rearrange("l (g p t) -> p (l g) t", g=G, p=P, t=PACK)
+        )
+        bdec = const.tile([P, L * D], BF16, name="bdec")
+        x_codes = const.tile([P, L * T], U32, name="x_codes", align_bytes=64)
+        x_scales = const.tile([P, L * T], U8, name="x_scales", align_bytes=64)
+
+        enc_raw = {}
+        enc_banks = {}
+        enc_grouped = {}
+        enc_codes = {0: (x_codes, x_scales)}
+        enc_out = {}
+        biased = {}
+        acts = {}
+        act_codes = {}
+        dec_raw = {}
+        dec_grouped = {}
+        dec_codes = {}
+        acc = {}
+
+        def load_enc(n):
+            if n == 0:
+                raw = const.tile([P, L, D], BF16, name="x_raw")
+                src = x.rearrange("l t k -> t l k")
+            else:
+                raw = rawp.tile([P, PACK, KP], BF16, name="raw", tag="raw")
+                l, g = enc_chunks[n]
+                src = W_enc[l, g * KP : (g + 1) * KP, :].rearrange("(m t) k -> m t k", t=PACK)
+            nc.sync.dma_start(out=raw[:], in_=src)
+            enc_raw[n] = raw
+
+        def load_dec(c):
+            i, j, g = dec_chunks[c]
+            raw = rawp.tile([P, PACK, D], BF16, name="raw", tag="raw")
+            nc.sync.dma_start(
+                out=raw[:],
+                in_=W_dec[i, j, g * KP : (g + 1) * KP, :].rearrange("(p t) d -> p t d", t=PACK),
+            )
+            dec_raw[c] = raw
+
+        def load_group(r):
+            if r < n_pairs:
+                load_dec(2 * r)
+                load_dec(2 * r + 1)
+                if r == 0:
+                    load_enc(0)
+            if r == BDEC_GROUP:
+                nc.sync.dma_start(
+                    out=bdec[:], in_=b_dec.rearrange("l d -> (l d)").partition_broadcast(P)
+                )
+            if r + 1 < n_enc:
+                load_enc(r + 1)
+
+        def transposes(n):
+            raw = enc_raw[n]
+            banks = []
+            for h in range(2):
+                tp = tpp.tile([P, 2, 2, P], F32, name="tp", tag="tp")
+                for s in range(2):
+                    words = raw[:, 2 * h + s, :].bitcast(F32)
+                    for u in range(2):
+                        nc.tensor.transpose(tp[:, s, u, :], words[:, u : KP // 2 : 2], ident[:])
+                banks.append(tp)
+            enc_banks[n] = banks
+
+        def evacuate(n):
+            wg = wgp.tile([P, PACK, P, PACK], BF16, name="wg", tag="wg", align_bytes=64)
+            wg_words = wg[:].bitcast(F32)
+            for h in range(2):
+                nc.scalar.copy(
+                    out=wg_words[:, 2 * h : 2 * h + 2, :, :],
+                    in_=enc_banks[n][h][:].rearrange("p s u m -> p s m u"),
+                )
+            enc_grouped[n] = wg
+
+        def quant_w(n):
+            if n > 0:
+                codes = wcp.tile([P, KP], U32, name="w_codes", tag="w_codes", align_bytes=64)
+                scales = wcp.tile([P, KP], U8, name="w_scales", tag="w_scales", align_bytes=64)
+                enc_codes[n] = (codes, scales)
+            codes, scales = enc_codes[n]
+            nc.vector.quantize_mx(
+                out=codes[:].bitcast(FP8X4),
+                scales=scales[:],
+                in_=enc_grouped[n][:].rearrange("p s m j -> p (s m j)"),
+            )
+
+        def enc_mm(n):
+            l, g = enc_chunks[n]
+            codes, scales = enc_codes[n]
+            ep = epp.tile([P, PACK, T], BANK_DT, name="ep", tag="ep")
+            for t in range(PACK):
+                nc.tensor.matmul_mx(
+                    out=ep[:, t, :],
+                    lhsT=codes[:, t * P : (t + 1) * P].bitcast(FP8X4),
+                    lhsT_scale=scales[:, t * P : (t + 1) * P],
+                    rhs=x_codes[:, l * T : (l + 1) * T].bitcast(FP8X4),
+                    rhs_scale=x_scales[:, l * T : (l + 1) * T],
+                    start=True,
+                    stop=True,
+                )
+            enc_out[n] = ep
+
+        def bias_add(n):
+            l, g = enc_chunks[n]
+            if g == 0:
+                biased[l] = actp.tile([P, G, T, PACK], BF16, name="biased", tag="biased")
+            nc.vector.tensor_tensor(
+                out=biased[l][:, g, :, :],
+                in0=enc_out[n][:].rearrange("p t n -> p n t"),
+                in1=benc[:, n - 1 : n, :].to_broadcast([P, T, PACK]),
+                op=ADD,
+            )
+
+        def relu(l):
+            acts[l] = actp.tile([P, G * T * PACK], BF16, name="acts", tag="acts", align_bytes=64)
+            nc.vector.tensor_scalar_max(
+                out=acts[l][:], in0=biased[l][:].rearrange("p g n t -> p (g n t)"), scalar1=0.0
+            )
+
+        def quant_a(l):
+            codes = const.tile([P, G * T], U32, name="a_codes%d" % l, align_bytes=64)
+            scales = const.tile([P, G * T], U8, name="a_scales%d" % l, align_bytes=64)
+            for lo, hi in ((0, 2 * T), (2 * T, 3 * T)):
+                nc.vector.quantize_mx(
+                    out=codes[:, lo:hi].bitcast(FP8X4),
+                    scales=scales[:, lo:hi],
+                    in_=acts[l][:, lo * PACK : hi * PACK],
+                )
+            act_codes[l] = (codes, scales)
+
+        def interleave(r):
+            dg = dgp.tile([P, 2, D, PACK], BF16, name="dg", tag="dg", align_bytes=64)
+            dec_grouped[r] = dg
+            for h in range(2):
+                raw = dec_raw[2 * r + h]
+                sc = S_COLS[r][h]
+                if sc > 0:
+                    nc.scalar.copy(
+                        out=dg[:, h, 0:sc, :], in_=raw[:, :, 0:sc].rearrange("p t d -> p d t")
+                    )
+                if sc < D:
+                    nc.vector.tensor_copy(
+                        out=dg[:, h, sc:D, :], in_=raw[:, :, sc:D].rearrange("p t d -> p d t")
+                    )
+
+        def quant_d(r):
+            codes = dcp.tile([P, 2 * D], U32, name="d_codes", tag="d_codes", align_bytes=64)
+            scales = dcp.tile([P, 2 * D], U8, name="d_scales", tag="d_scales", align_bytes=64)
+            nc.vector.quantize_mx(
+                out=codes[:].bitcast(FP8X4),
+                scales=scales[:],
+                in_=dec_grouped[r][:].rearrange("p h d t -> p (h d t)"),
+            )
+            dec_codes[r] = (codes, scales)
+
+        def dec_mm(r):
+            closed = []
+            codes, scales = dec_codes[r]
+            for h in range(2):
+                i, j, g = dec_chunks[2 * r + h]
+                if i == 0 and g == 0:
+                    acc[j] = accp.tile([P, D], F32, name="acc%d" % j)
+                a_codes, a_scales = act_codes[i]
+                nc.tensor.matmul_mx(
+                    out=acc[j][:],
+                    lhsT=a_codes[:, g * T : (g + 1) * T].bitcast(FP8X4),
+                    lhsT_scale=a_scales[:, g * T : (g + 1) * T],
+                    rhs=codes[:, h * D : (h + 1) * D].bitcast(FP8X4),
+                    rhs_scale=scales[:, h * D : (h + 1) * D],
+                    start=(i == 0 and g == 0),
+                    stop=(i == j and g == G - 1),
+                )
+                if i == j and g == G - 1:
+                    closed.append(j)
+            return closed
+
+        def epilogue(j):
+            ot = otp.tile([P, D], F32, name="ot", tag="ot")
+            nc.vector.tensor_tensor(
+                out=ot[:], in0=acc[j][:], in1=bdec[:, j * D : (j + 1) * D], op=ADD
+            )
+            nc.sync.dma_start(out=out[j], in_=ot[:])
+
+        for r in range(LOOKAHEAD):
+            load_group(r)
+        transposes(0)
+
+        next_pair = 0
+        due = {}
+        for r in range(n_pairs + 1):
+            load_group(r + LOOKAHEAD)
+            n = r - 1
+            if r < n_enc:
+                evacuate(r)
+            if 0 <= n < n_enc:
+                quant_w(n)
+            if 1 <= n < n_enc:
+                enc_mm(n)
+            if r + 1 < n_enc:
+                transposes(r + 1)
+            layer_done = (r - 5) // G if (r >= 5 and (r - 5) % G == 0 and (r - 5) // G < L) else None
+            if layer_done is not None:
+                relu(layer_done)
+            if r < n_pairs:
+                interleave(r)
+            if r >= 1:
+                quant_d(r - 1)
+            if layer_done is not None:
+                quant_a(layer_done)
+            written = 0
+            while written < 2 and next_pair < r and all(
+                dec_chunks[2 * next_pair + h][0] in act_codes for h in range(2)
+            ):
+                for j in dec_mm(next_pair):
+                    when = r if r == n_pairs else max(r + 1, FIRST_EPILOGUE_ROUND)
+                    due.setdefault(when, []).append(j)
+                next_pair += 1
+                written += 1
+            if 1 <= n < n_enc:
+                bias_add(n)
+            for j in due.get(r, []):
+                epilogue(j)

@@ -20,8 +20,8 @@ BANK_DT = F32
 FLOPS = 2 * L * T * F * D + 2 * 10 * T * F * D
 BYTES = 2 * (L * T * D + L * F * D + L * F + L * D + 10 * F * D) + 4 * L * T * D
 
-LOOKAHEAD = 3
-BDEC_GROUP = 6
+LOOKAHEAD = 4
+BDEC_GROUP = 7
 FIRST_EPILOGUE_ROUND = 8
 S_COLS = [[192, 0], [448, 0], [512, 0], [512, 0], [512, 0], [512, 144], [512, 0], [512, 0], [512, 224], [512, 96], [512, 0], [512, 144], [512, 0], [512, 256], [512, 144]]
 
@@ -49,10 +49,9 @@ def tile_crosslayertranscoder_kernel(tc, x, W_enc, b_enc, b_dec, W_dec, dec_mask
 
         ident = const.tile([P, P], F32, name="ident")
         make_identity(nc, ident[:])
+        benc_rows = const.tile([P, KP], BF16, name="benc_rows")
+        nc.gpsimd.memset(benc_rows[:], 0.0)
         benc = const.tile([P, L * G, PACK], BF16, name="benc")
-        nc.scalar.dma_start(
-            out=benc[:], in_=b_enc.rearrange("l (g p t) -> p (l g) t", g=G, p=P, t=PACK)
-        )
         bdec = const.tile([P, L * D], BF16, name="bdec")
         x_codes = const.tile([P, L * T], U32, name="x_codes", align_bytes=64)
         x_scales = const.tile([P, L * T], U8, name="x_scales", align_bytes=64)
@@ -92,10 +91,10 @@ def tile_crosslayertranscoder_kernel(tc, x, W_enc, b_enc, b_dec, W_dec, dec_mask
 
         def load_group(r):
             if r < n_pairs:
-                load_dec(2 * r)
-                load_dec(2 * r + 1)
                 if r == 0:
                     load_enc(0)
+                load_dec(2 * r)
+                load_dec(2 * r + 1)
             if r == BDEC_GROUP:
                 nc.sync.dma_start(
                     out=bdec[:], in_=b_dec.rearrange("l d -> (l d)").partition_broadcast(P)
@@ -189,11 +188,13 @@ def tile_crosslayertranscoder_kernel(tc, x, W_enc, b_enc, b_dec, W_dec, dec_mask
                 sc = S_COLS[r][h]
                 if sc > 0:
                     nc.scalar.copy(
-                        out=dg[:, h, 0:sc, :], in_=raw[:, :, 0:sc].rearrange("p t d -> p d t")
+                        out=dg[:, h, 0:sc, :].rearrange("p (c i) t -> p c t i", i=4),
+                        in_=raw[:, :, 0:sc].rearrange("p t (c i) -> p c t i", i=4),
                     )
                 if sc < D:
                     nc.vector.tensor_copy(
-                        out=dg[:, h, sc:D, :], in_=raw[:, :, sc:D].rearrange("p t d -> p d t")
+                        out=dg[:, h, sc:D, :].rearrange("p (c i) t -> p c t i", i=4),
+                        in_=raw[:, :, sc:D].rearrange("p t (c i) -> p c t i", i=4),
                     )
 
         def quant_d(r):
@@ -236,7 +237,15 @@ def tile_crosslayertranscoder_kernel(tc, x, W_enc, b_enc, b_dec, W_dec, dec_mask
 
         for r in range(LOOKAHEAD):
             load_group(r)
+        nc.scalar.dma_start(
+            out=benc_rows[0 : L * G, :], in_=b_enc.rearrange("l (g c) -> (l g) c", g=G)
+        )
         transposes(0)
+        benc_bank = epp.tile([P, 2, P], F32, name="benc_bank", tag="ep")
+        for u in range(2):
+            nc.tensor.transpose(
+                benc_bank[:, u, :], benc_rows[:].bitcast(F32)[:, u : KP // 2 : 2], ident[:]
+            )
 
         next_pair = 0
         due = {}
@@ -256,6 +265,11 @@ def tile_crosslayertranscoder_kernel(tc, x, W_enc, b_enc, b_dec, W_dec, dec_mask
                 relu(layer_done)
             if r < n_pairs:
                 interleave(r)
+            if r == 0:
+                nc.vector.tensor_copy(
+                    out=benc[:].bitcast(F32),
+                    in_=benc_bank[:, :, 0 : L * G].rearrange("p u e -> p e u"),
+                )
             if r >= 1:
                 quant_d(r - 1)
             if layer_done is not None:

@@ -13,17 +13,25 @@ ADD = mybir.AluOpType.add
 L, T, F, D = 4, 128, 1536, 512
 P = 128
 PACK = 4
-KP = P * PACK
-G = F // KP
-BANK_DT = F32
+K_PASS = P * PACK
+G = F // K_PASS
+HALF = D // 2
+ENC_BANK = F32
 
-FLOPS = 2 * L * T * F * D + 2 * 10 * T * F * D
-BYTES = 2 * (L * T * D + L * F * D + L * F + L * D + 10 * F * D) + 4 * L * T * D
+N_BLOCKS = L * (L + 1) // 2
+FLOPS = 2 * L * T * F * D + 2 * N_BLOCKS * T * F * D
+BYTES = 2 * (L * T * D + L * F * D + L * F + L * D + N_BLOCKS * F * D) + 4 * L * T * D
 
 LOOKAHEAD = 4
-BDEC_GROUP = 7
-FIRST_EPILOGUE_ROUND = 8
-S_COLS = [[192, 0], [448, 0], [512, 0], [512, 0], [512, 0], [512, 144], [512, 0], [512, 0], [512, 224], [512, 96], [512, 0], [512, 144], [512, 0], [512, 256], [512, 144]]
+BDEC_ROUND = 7
+FIRST_OUTPUT_ROUND = BDEC_ROUND + 1
+MAX_PAIRS_A_ROUND = 2
+RUN = 4
+SCALAR_COLUMNS = (
+    [(192, 0), (448, 0), (512, 0), (512, 0), (512, 0)]
+    + [(512, 144), (512, 0), (512, 0), (512, 224), (512, 96)]
+    + [(512, 0), (512, 144), (512, 0), (512, 320), (512, 256)]
+)
 
 
 def tile_crosslayertranscoder_kernel(tc, x, W_enc, b_enc, b_dec, W_dec, dec_mask, out):
@@ -32,35 +40,38 @@ def tile_crosslayertranscoder_kernel(tc, x, W_enc, b_enc, b_dec, W_dec, dec_mask
     dec_chunks = [(i, j, g) for i in range(L) for j in range(i, L) for g in range(G)]
     n_enc = len(enc_chunks)
     n_pairs = len(dec_chunks) // 2
+    layer_finished_in = {G * l + G + 2: l for l in range(L)}
 
     with ExitStack() as ctx:
-        const = ctx.enter_context(tc.tile_pool(name="const", bufs=1))
-        rawp = ctx.enter_context(tc.tile_pool(name="rawp", bufs=3 * (LOOKAHEAD + 1)))
-        wgp = ctx.enter_context(tc.tile_pool(name="wgp", bufs=2))
-        wcp = ctx.enter_context(tc.tile_pool(name="wcp", bufs=2))
-        dgp = ctx.enter_context(tc.tile_pool(name="dgp", bufs=3))
-        dcp = ctx.enter_context(tc.tile_pool(name="dcp", bufs=5))
-        actp = ctx.enter_context(tc.tile_pool(name="actp", bufs=2))
-        otp = ctx.enter_context(tc.tile_pool(name="otp", bufs=2))
-        tpp = ctx.enter_context(tc.psum_pool(name="tpp", bufs=2))
-        epp = ctx.enter_context(tc.psum_pool(name="epp", bufs=2))
-        accp = ctx.enter_context(tc.psum_pool(name="accp", bufs=1))
+        keep = ctx.enter_context(tc.tile_pool(name="keep", bufs=1))
+        raw_pool = ctx.enter_context(tc.tile_pool(name="raw_pool", bufs=3 * (LOOKAHEAD + 1)))
+        enc_pool = ctx.enter_context(tc.tile_pool(name="enc_pool", bufs=2))
+        act_pool = ctx.enter_context(tc.tile_pool(name="act_pool", bufs=2))
+        out_pool = ctx.enter_context(tc.tile_pool(name="out_pool", bufs=2))
+        grouped_pool = ctx.enter_context(tc.tile_pool(name="grouped_pool", bufs=3))
+        code_pool = ctx.enter_context(tc.tile_pool(name="code_pool", bufs=5))
+        turn_pool = ctx.enter_context(tc.psum_pool(name="turn_pool", bufs=2))
+        bank_pool = ctx.enter_context(tc.psum_pool(name="bank_pool", bufs=1))
+        acc_pool = ctx.enter_context(tc.psum_pool(name="acc_pool", bufs=1))
         ctx.enter_context(tc.manual_schedule())
 
-        ident = const.tile([P, P], F32, name="ident")
-        make_identity(nc, ident[:])
-        benc_rows = const.tile([P, KP], BF16, name="benc_rows")
+        benc_rows = keep.tile([P, K_PASS], BF16, name="benc_rows")
         nc.gpsimd.memset(benc_rows[:], 0.0)
-        benc = const.tile([P, L * G, PACK], BF16, name="benc")
-        bdec = const.tile([P, L * D], BF16, name="bdec")
-        x_codes = const.tile([P, L * T], U32, name="x_codes", align_bytes=64)
-        x_scales = const.tile([P, L * T], U8, name="x_scales", align_bytes=64)
+        nc.scalar.dma_start(
+            out=benc_rows[0 : L * G, :], in_=b_enc.rearrange("l (g c) -> (l g) c", g=G)
+        )
+        ident = keep.tile([P, P], F32, name="ident")
+        make_identity(nc, ident[:])
+        benc = keep.tile([P, L * G, PACK], BF16, name="benc")
+        bdec = keep.tile([P, L * D], BF16, name="bdec")
+        x_codes = keep.tile([P, L * T], U32, name="x_codes", align_bytes=64)
+        x_scales = keep.tile([P, L * T], U8, name="x_scales", align_bytes=64)
 
         enc_raw = {}
-        enc_banks = {}
+        enc_turned = {}
         enc_grouped = {}
         enc_codes = {0: (x_codes, x_scales)}
-        enc_out = {}
+        enc_bank = {}
         biased = {}
         acts = {}
         act_codes = {}
@@ -68,110 +79,124 @@ def tile_crosslayertranscoder_kernel(tc, x, W_enc, b_enc, b_dec, W_dec, dec_mask
         dec_grouped = {}
         dec_codes = {}
         acc = {}
+        staged = {}
 
         def load_enc(n):
             if n == 0:
-                raw = const.tile([P, L, D], BF16, name="x_raw")
-                src = x.rearrange("l t k -> t l k")
+                raw = keep.tile([P, L, D], BF16, name="x_raw")
+                rows = x.rearrange("l t k -> t l k")
             else:
-                raw = rawp.tile([P, PACK, KP], BF16, name="raw", tag="raw")
+                raw = raw_pool.tile([P, PACK, D], BF16, name="raw", tag="raw")
                 l, g = enc_chunks[n]
-                src = W_enc[l, g * KP : (g + 1) * KP, :].rearrange("(m t) k -> m t k", t=PACK)
-            nc.sync.dma_start(out=raw[:], in_=src)
+                rows = W_enc[l, g * K_PASS : (g + 1) * K_PASS, :].rearrange(
+                    "(m s) k -> m s k", s=PACK
+                )
+            nc.sync.dma_start(out=raw[:], in_=rows)
             enc_raw[n] = raw
 
         def load_dec(c):
             i, j, g = dec_chunks[c]
-            raw = rawp.tile([P, PACK, D], BF16, name="raw", tag="raw")
+            raw = raw_pool.tile([P, PACK, D], BF16, name="raw", tag="raw")
             nc.sync.dma_start(
                 out=raw[:],
-                in_=W_dec[i, j, g * KP : (g + 1) * KP, :].rearrange("(p t) d -> p t d", t=PACK),
+                in_=W_dec[i, j, g * K_PASS : (g + 1) * K_PASS, :].rearrange(
+                    "(p t) d -> p t d", t=PACK
+                ),
             )
             dec_raw[c] = raw
 
-        def load_group(r):
+        def load_for_round(r):
+            if r == 0:
+                load_enc(0)
             if r < n_pairs:
-                if r == 0:
-                    load_enc(0)
                 load_dec(2 * r)
                 load_dec(2 * r + 1)
-            if r == BDEC_GROUP:
+            if r == BDEC_ROUND:
                 nc.sync.dma_start(
                     out=bdec[:], in_=b_dec.rearrange("l d -> (l d)").partition_broadcast(P)
                 )
             if r + 1 < n_enc:
                 load_enc(r + 1)
 
-        def transposes(n):
-            raw = enc_raw[n]
+        def every_2nd_word(row_of_k, u):
+            return row_of_k.bitcast(F32)[:, u : D // 2 : 2]
+
+        def transpose_chunk(n):
             banks = []
             for h in range(2):
-                tp = tpp.tile([P, 2, 2, P], F32, name="tp", tag="tp")
+                turned = turn_pool.tile([P, 2, 2, P], F32, name="turned", tag="turned")
                 for s in range(2):
-                    words = raw[:, 2 * h + s, :].bitcast(F32)
                     for u in range(2):
-                        nc.tensor.transpose(tp[:, s, u, :], words[:, u : KP // 2 : 2], ident[:])
-                banks.append(tp)
-            enc_banks[n] = banks
+                        nc.tensor.transpose(
+                            turned[:, s, u, :],
+                            every_2nd_word(enc_raw[n][:, 2 * h + s, :], u),
+                            ident[:],
+                        )
+                banks.append(turned)
+            enc_turned[n] = banks
 
-        def evacuate(n):
-            wg = wgp.tile([P, PACK, P, PACK], BF16, name="wg", tag="wg", align_bytes=64)
-            wg_words = wg[:].bitcast(F32)
+        def empty_transposes(n):
+            grouped = enc_pool.tile(
+                [P, PACK, P, PACK], BF16, name="enc_grouped", tag="enc_grouped", align_bytes=64
+            )
+            words = grouped[:].bitcast(F32)
             for h in range(2):
                 nc.scalar.copy(
-                    out=wg_words[:, 2 * h : 2 * h + 2, :, :],
-                    in_=enc_banks[n][h][:].rearrange("p s u m -> p s m u"),
+                    out=words[:, 2 * h : 2 * h + 2, :, :],
+                    in_=enc_turned[n][h][:].rearrange("q s u m -> q s m u"),
                 )
-            enc_grouped[n] = wg
+            enc_grouped[n] = grouped
 
-        def quant_w(n):
+        def quantize_chunk(n):
             if n > 0:
-                codes = wcp.tile([P, KP], U32, name="w_codes", tag="w_codes", align_bytes=64)
-                scales = wcp.tile([P, KP], U8, name="w_scales", tag="w_scales", align_bytes=64)
+                codes = enc_pool.tile([P, K_PASS], U32, name="w_codes", tag="w_codes", align_bytes=64)
+                scales = enc_pool.tile(
+                    [P, K_PASS], U8, name="w_scales", tag="w_scales", align_bytes=64
+                )
                 enc_codes[n] = (codes, scales)
             codes, scales = enc_codes[n]
             nc.vector.quantize_mx(
                 out=codes[:].bitcast(FP8X4),
                 scales=scales[:],
-                in_=enc_grouped[n][:].rearrange("p s m j -> p (s m j)"),
+                in_=enc_grouped[n][:].rearrange("q s m j -> q (s m j)"),
             )
 
-        def enc_mm(n):
+        def encode_chunk(n):
             l, g = enc_chunks[n]
             codes, scales = enc_codes[n]
-            ep = epp.tile([P, PACK, T], BANK_DT, name="ep", tag="ep")
-            for t in range(PACK):
+            bank = bank_pool.tile([P, PACK, T], ENC_BANK, name="bank", tag="bank")
+            for s in range(PACK):
                 nc.tensor.matmul_mx(
-                    out=ep[:, t, :],
-                    lhsT=codes[:, t * P : (t + 1) * P].bitcast(FP8X4),
-                    lhsT_scale=scales[:, t * P : (t + 1) * P],
+                    out=bank[:, s, :],
+                    lhsT=codes[:, s * P : (s + 1) * P].bitcast(FP8X4),
+                    lhsT_scale=scales[:, s * P : (s + 1) * P],
                     rhs=x_codes[:, l * T : (l + 1) * T].bitcast(FP8X4),
                     rhs_scale=x_scales[:, l * T : (l + 1) * T],
                     start=True,
                     stop=True,
                 )
-            enc_out[n] = ep
+            enc_bank[n] = bank
 
-        def bias_add(n):
+        def add_benc(n):
             l, g = enc_chunks[n]
             if g == 0:
-                biased[l] = actp.tile([P, G, T, PACK], BF16, name="biased", tag="biased")
+                biased[l] = act_pool.tile([P, G, T, PACK], BF16, name="biased", tag="biased")
             nc.vector.tensor_tensor(
                 out=biased[l][:, g, :, :],
-                in0=enc_out[n][:].rearrange("p t n -> p n t"),
+                in0=enc_bank[n][:].rearrange("p s n -> p n s"),
                 in1=benc[:, n - 1 : n, :].to_broadcast([P, T, PACK]),
                 op=ADD,
             )
 
-        def relu(l):
-            acts[l] = actp.tile([P, G * T * PACK], BF16, name="acts", tag="acts", align_bytes=64)
+        def relu_layer(l):
+            acts[l] = act_pool.tile([P, G * T * PACK], BF16, name="acts", tag="acts", align_bytes=64)
             nc.vector.tensor_scalar_max(
-                out=acts[l][:], in0=biased[l][:].rearrange("p g n t -> p (g n t)"), scalar1=0.0
+                out=acts[l][:], in0=biased[l][:].rearrange("p g n s -> p (g n s)"), scalar1=0.0
             )
 
-        def quant_a(l):
-            codes = const.tile([P, G * T], U32, name="a_codes%d" % l, align_bytes=64)
-            scales = const.tile([P, G * T], U8, name="a_scales%d" % l, align_bytes=64)
+        def quantize_acts(l):
+            codes = keep.tile([P, G * T], U32, name="a_codes%d" % l, align_bytes=64)
+            scales = keep.tile([P, G * T], U8, name="a_scales%d" % l, align_bytes=64)
             for lo, hi in ((0, 2 * T), (2 * T, 3 * T)):
                 nc.vector.quantize_mx(
                     out=codes[:, lo:hi].bitcast(FP8X4),
@@ -180,110 +205,131 @@ def tile_crosslayertranscoder_kernel(tc, x, W_enc, b_enc, b_dec, W_dec, dec_mask
                 )
             act_codes[l] = (codes, scales)
 
-        def interleave(r):
-            dg = dgp.tile([P, 2, D, PACK], BF16, name="dg", tag="dg", align_bytes=64)
-            dec_grouped[r] = dg
+        def interleave_columns(engine_copy, grouped, h, raw, lo, hi):
+            engine_copy(
+                out=grouped[:, h, lo:hi, :].rearrange("p (c i) t -> p c t i", i=RUN),
+                in_=raw[:, :, lo:hi].rearrange("p t (c i) -> p c t i", i=RUN),
+            )
+
+        def interleave_pair(r):
+            grouped = grouped_pool.tile(
+                [P, 2, D, PACK], BF16, name="dec_grouped", tag="dec_grouped", align_bytes=64
+            )
+            dec_grouped[r] = grouped
             for h in range(2):
                 raw = dec_raw[2 * r + h]
-                sc = S_COLS[r][h]
-                if sc > 0:
-                    nc.scalar.copy(
-                        out=dg[:, h, 0:sc, :].rearrange("p (c i) t -> p c t i", i=4),
-                        in_=raw[:, :, 0:sc].rearrange("p t (c i) -> p c t i", i=4),
-                    )
-                if sc < D:
-                    nc.vector.tensor_copy(
-                        out=dg[:, h, sc:D, :].rearrange("p (c i) t -> p c t i", i=4),
-                        in_=raw[:, :, sc:D].rearrange("p t (c i) -> p c t i", i=4),
-                    )
+                split = SCALAR_COLUMNS[r][h]
+                if split > 0:
+                    interleave_columns(nc.scalar.copy, grouped, h, raw, 0, split)
+                if split < D:
+                    interleave_columns(nc.vector.tensor_copy, grouped, h, raw, split, D)
 
-        def quant_d(r):
-            codes = dcp.tile([P, 2 * D], U32, name="d_codes", tag="d_codes", align_bytes=64)
-            scales = dcp.tile([P, 2 * D], U8, name="d_scales", tag="d_scales", align_bytes=64)
-            nc.vector.quantize_mx(
-                out=codes[:].bitcast(FP8X4),
-                scales=scales[:],
-                in_=dec_grouped[r][:].rearrange("p h d t -> p (h d t)"),
-            )
-            dec_codes[r] = (codes, scales)
+        def quantize_pair(r, pieces):
+            if r not in dec_codes:
+                codes = code_pool.tile([P, 2 * D], U32, name="d_codes", tag="d_codes", align_bytes=64)
+                scales = code_pool.tile(
+                    [P, 2 * D], U8, name="d_scales", tag="d_scales", align_bytes=64
+                )
+                dec_codes[r] = (codes, scales)
+            codes, scales = dec_codes[r]
+            grouped = dec_grouped[r][:].rearrange("p h d t -> p (h d t)")
+            for lo, hi in pieces:
+                nc.vector.quantize_mx(
+                    out=codes[:, lo:hi].bitcast(FP8X4),
+                    scales=scales[:, lo:hi],
+                    in_=grouped[:, lo * PACK : hi * PACK],
+                )
 
-        def dec_mm(r):
+        def decode_pair(r):
             closed = []
             codes, scales = dec_codes[r]
             for h in range(2):
                 i, j, g = dec_chunks[2 * r + h]
-                if i == 0 and g == 0:
-                    acc[j] = accp.tile([P, D], F32, name="acc%d" % j)
+                first = i == 0 and g == 0
+                final = i == j and g == G - 1
+                parts = ((0, D),) if j < L - 1 else ((HALF, D), (0, HALF))
                 a_codes, a_scales = act_codes[i]
-                nc.tensor.matmul_mx(
-                    out=acc[j][:],
-                    lhsT=a_codes[:, g * T : (g + 1) * T].bitcast(FP8X4),
-                    lhsT_scale=a_scales[:, g * T : (g + 1) * T],
-                    rhs=codes[:, h * D : (h + 1) * D].bitcast(FP8X4),
-                    rhs_scale=scales[:, h * D : (h + 1) * D],
-                    start=(i == 0 and g == 0),
-                    stop=(i == j and g == G - 1),
-                )
-                if i == j and g == G - 1:
-                    closed.append(j)
+                for lo, hi in parts:
+                    if first:
+                        acc[(j, lo)] = acc_pool.tile([P, hi - lo], F32, name="acc%d_%d" % (j, lo))
+                    nc.tensor.matmul_mx(
+                        out=acc[(j, lo)][:],
+                        lhsT=a_codes[:, g * T : (g + 1) * T].bitcast(FP8X4),
+                        lhsT_scale=a_scales[:, g * T : (g + 1) * T],
+                        rhs=codes[:, h * D + lo : h * D + hi].bitcast(FP8X4),
+                        rhs_scale=scales[:, h * D + lo : h * D + hi],
+                        start=first,
+                        stop=final,
+                    )
+                    if final:
+                        closed.append((j, lo, hi))
             return closed
 
-        def epilogue(j):
-            ot = otp.tile([P, D], F32, name="ot", tag="ot")
+        def add_bdec_and_store(j, lo, hi):
+            if j not in staged:
+                staged[j] = out_pool.tile([P, D], F32, name="staged", tag="staged")
             nc.vector.tensor_tensor(
-                out=ot[:], in0=acc[j][:], in1=bdec[:, j * D : (j + 1) * D], op=ADD
+                out=staged[j][:, lo:hi],
+                in0=acc[(j, lo)][:],
+                in1=bdec[:, j * D + lo : j * D + hi],
+                op=ADD,
             )
-            nc.sync.dma_start(out=out[j], in_=ot[:])
+            if lo == 0:
+                nc.sync.dma_start(out=out[j], in_=staged[j][:])
 
+        benc_turned = bank_pool.tile([P, 2, P], F32, name="benc_turned", tag="bank")
         for r in range(LOOKAHEAD):
-            load_group(r)
-        nc.scalar.dma_start(
-            out=benc_rows[0 : L * G, :], in_=b_enc.rearrange("l (g c) -> (l g) c", g=G)
-        )
-        transposes(0)
-        benc_bank = epp.tile([P, 2, P], F32, name="benc_bank", tag="ep")
-        for u in range(2):
-            nc.tensor.transpose(
-                benc_bank[:, u, :], benc_rows[:].bitcast(F32)[:, u : KP // 2 : 2], ident[:]
-            )
+            load_for_round(r)
+        transpose_chunk(0)
 
         next_pair = 0
-        due = {}
+        outputs_due = {}
         for r in range(n_pairs + 1):
-            load_group(r + LOOKAHEAD)
+            load_for_round(r + LOOKAHEAD)
             n = r - 1
+            finished = layer_finished_in.get(r)
             if r < n_enc:
-                evacuate(r)
+                empty_transposes(r)
             if 0 <= n < n_enc:
-                quant_w(n)
+                quantize_chunk(n)
             if 1 <= n < n_enc:
-                enc_mm(n)
+                encode_chunk(n)
             if r + 1 < n_enc:
-                transposes(r + 1)
-            layer_done = (r - 5) // G if (r >= 5 and (r - 5) % G == 0 and (r - 5) // G < L) else None
-            if layer_done is not None:
-                relu(layer_done)
+                transpose_chunk(r + 1)
+            if r == 1:
+                for u in range(2):
+                    nc.tensor.transpose(
+                        benc_turned[:, u, :], every_2nd_word(benc_rows[:], u), ident[:]
+                    )
+            if finished is not None:
+                relu_layer(finished)
             if r < n_pairs:
-                interleave(r)
-            if r == 0:
+                interleave_pair(r)
+            if 1 <= r < n_pairs:
+                quantize_pair(r - 1, ((0, 2 * D),))
+            if r == n_pairs:
+                quantize_pair(r - 1, ((0, D),))
+            if r == 1:
                 nc.vector.tensor_copy(
                     out=benc[:].bitcast(F32),
-                    in_=benc_bank[:, :, 0 : L * G].rearrange("p u e -> p e u"),
+                    in_=benc_turned[:, :, 0 : L * G].rearrange("p u c -> p c u"),
                 )
-            if r >= 1:
-                quant_d(r - 1)
-            if layer_done is not None:
-                quant_a(layer_done)
+            if finished is not None:
+                quantize_acts(finished)
+            if r == n_pairs:
+                quantize_pair(r - 1, ((D + HALF, 2 * D), (D, D + HALF)))
             written = 0
-            while written < 2 and next_pair < r and all(
-                dec_chunks[2 * next_pair + h][0] in act_codes for h in range(2)
+            while (
+                written < MAX_PAIRS_A_ROUND
+                and next_pair < r
+                and all(dec_chunks[2 * next_pair + h][0] in act_codes for h in range(2))
             ):
-                for j in dec_mm(next_pair):
-                    when = r if r == n_pairs else max(r + 1, FIRST_EPILOGUE_ROUND)
-                    due.setdefault(when, []).append(j)
+                for group in decode_pair(next_pair):
+                    when = r if r == n_pairs else max(r + 1, FIRST_OUTPUT_ROUND)
+                    outputs_due.setdefault(when, []).append(group)
                 next_pair += 1
                 written += 1
             if 1 <= n < n_enc:
-                bias_add(n)
-            for j in due.get(r, []):
-                epilogue(j)
+                add_benc(n)
+            for j, lo, hi in outputs_due.get(r, []):
+                add_bdec_and_store(j, lo, hi)

from contextlib import ExitStack

import concourse.mybir as mybir
from concourse.masks import make_identity

F32 = mybir.dt.float32
BF16 = mybir.dt.bfloat16
U32 = mybir.dt.uint32
U8 = mybir.dt.uint8
FP8X4 = mybir.dt.float8_e4m3fn_x4
ADD = mybir.AluOpType.add

L, T, F, D = 4, 128, 1536, 512
P = 128
PACK = 4
K_PASS = P * PACK
G = F // K_PASS
HALF = D // 2
ENC_BANK = F32

N_BLOCKS = L * (L + 1) // 2
FLOPS = 2 * L * T * F * D + 2 * N_BLOCKS * T * F * D
BYTES = 2 * (L * T * D + L * F * D + L * F + L * D + N_BLOCKS * F * D) + 4 * L * T * D

LOOKAHEAD = 4
BDEC_ROUND = 7
FIRST_OUTPUT_ROUND = BDEC_ROUND + 1
MAX_PAIRS_A_ROUND = 2
RUN = 4
SCALAR_COLUMNS = (
    [(192, 0), (448, 0), (512, 0), (512, 0), (512, 0)]
    + [(512, 144), (512, 0), (512, 0), (512, 224), (512, 96)]
    + [(512, 0), (512, 144), (512, 0), (512, 320), (512, 256)]
)


def tile_crosslayertranscoder_kernel(tc, x, W_enc, b_enc, b_dec, W_dec, dec_mask, out):
    nc = tc.nc
    enc_chunks = [None] + [(l, g) for l in range(L) for g in range(G)]
    dec_chunks = [(i, j, g) for i in range(L) for j in range(i, L) for g in range(G)]
    n_enc = len(enc_chunks)
    n_pairs = len(dec_chunks) // 2
    layer_finished_in = {G * l + G + 2: l for l in range(L)}

    with ExitStack() as ctx:
        keep = ctx.enter_context(tc.tile_pool(name="keep", bufs=1))
        raw_pool = ctx.enter_context(tc.tile_pool(name="raw_pool", bufs=3 * (LOOKAHEAD + 1)))
        enc_pool = ctx.enter_context(tc.tile_pool(name="enc_pool", bufs=2))
        act_pool = ctx.enter_context(tc.tile_pool(name="act_pool", bufs=2))
        out_pool = ctx.enter_context(tc.tile_pool(name="out_pool", bufs=2))
        grouped_pool = ctx.enter_context(tc.tile_pool(name="grouped_pool", bufs=3))
        code_pool = ctx.enter_context(tc.tile_pool(name="code_pool", bufs=5))
        turn_pool = ctx.enter_context(tc.psum_pool(name="turn_pool", bufs=2))
        bank_pool = ctx.enter_context(tc.psum_pool(name="bank_pool", bufs=1))
        acc_pool = ctx.enter_context(tc.psum_pool(name="acc_pool", bufs=1))
        ctx.enter_context(tc.manual_schedule())

        benc_rows = keep.tile([P, K_PASS], BF16, name="benc_rows")
        nc.gpsimd.memset(benc_rows[:], 0.0)
        nc.scalar.dma_start(
            out=benc_rows[0 : L * G, :], in_=b_enc.rearrange("l (g c) -> (l g) c", g=G)
        )
        ident = keep.tile([P, P], F32, name="ident")
        make_identity(nc, ident[:])
        benc = keep.tile([P, L * G, PACK], BF16, name="benc")
        bdec = keep.tile([P, L * D], BF16, name="bdec")
        x_codes = keep.tile([P, L * T], U32, name="x_codes", align_bytes=64)
        x_scales = keep.tile([P, L * T], U8, name="x_scales", align_bytes=64)

        enc_raw = {}
        enc_turned = {}
        enc_grouped = {}
        enc_codes = {0: (x_codes, x_scales)}
        enc_bank = {}
        biased = {}
        acts = {}
        act_codes = {}
        dec_raw = {}
        dec_grouped = {}
        dec_codes = {}
        acc = {}
        staged = {}

        def load_enc(n):
            if n == 0:
                raw = keep.tile([P, L, D], BF16, name="x_raw")
                rows = x.rearrange("l t k -> t l k")
            else:
                raw = raw_pool.tile([P, PACK, D], BF16, name="raw", tag="raw")
                l, g = enc_chunks[n]
                rows = W_enc[l, g * K_PASS : (g + 1) * K_PASS, :].rearrange(
                    "(m s) k -> m s k", s=PACK
                )
            nc.sync.dma_start(out=raw[:], in_=rows)
            enc_raw[n] = raw

        def load_dec(c):
            i, j, g = dec_chunks[c]
            raw = raw_pool.tile([P, PACK, D], BF16, name="raw", tag="raw")
            nc.sync.dma_start(
                out=raw[:],
                in_=W_dec[i, j, g * K_PASS : (g + 1) * K_PASS, :].rearrange(
                    "(p t) d -> p t d", t=PACK
                ),
            )
            dec_raw[c] = raw

        def load_for_round(r):
            if r == 0:
                load_enc(0)
            if r < n_pairs:
                load_dec(2 * r)
                load_dec(2 * r + 1)
            if r == BDEC_ROUND:
                nc.sync.dma_start(
                    out=bdec[:], in_=b_dec.rearrange("l d -> (l d)").partition_broadcast(P)
                )
            if r + 1 < n_enc:
                load_enc(r + 1)

        def every_2nd_word(row_of_k, u):
            return row_of_k.bitcast(F32)[:, u : D // 2 : 2]

        def transpose_chunk(n):
            banks = []
            for h in range(2):
                turned = turn_pool.tile([P, 2, 2, P], F32, name="turned", tag="turned")
                for s in range(2):
                    for u in range(2):
                        nc.tensor.transpose(
                            turned[:, s, u, :],
                            every_2nd_word(enc_raw[n][:, 2 * h + s, :], u),
                            ident[:],
                        )
                banks.append(turned)
            enc_turned[n] = banks

        def empty_transposes(n):
            grouped = enc_pool.tile(
                [P, PACK, P, PACK], BF16, name="enc_grouped", tag="enc_grouped", align_bytes=64
            )
            words = grouped[:].bitcast(F32)
            for h in range(2):
                nc.scalar.copy(
                    out=words[:, 2 * h : 2 * h + 2, :, :],
                    in_=enc_turned[n][h][:].rearrange("q s u m -> q s m u"),
                )
            enc_grouped[n] = grouped

        def quantize_chunk(n):
            if n > 0:
                codes = enc_pool.tile([P, K_PASS], U32, name="w_codes", tag="w_codes", align_bytes=64)
                scales = enc_pool.tile(
                    [P, K_PASS], U8, name="w_scales", tag="w_scales", align_bytes=64
                )
                enc_codes[n] = (codes, scales)
            codes, scales = enc_codes[n]
            nc.vector.quantize_mx(
                out=codes[:].bitcast(FP8X4),
                scales=scales[:],
                in_=enc_grouped[n][:].rearrange("q s m j -> q (s m j)"),
            )

        def encode_chunk(n):
            l, g = enc_chunks[n]
            codes, scales = enc_codes[n]
            bank = bank_pool.tile([P, PACK, T], ENC_BANK, name="bank", tag="bank")
            for s in range(PACK):
                nc.tensor.matmul_mx(
                    out=bank[:, s, :],
                    lhsT=codes[:, s * P : (s + 1) * P].bitcast(FP8X4),
                    lhsT_scale=scales[:, s * P : (s + 1) * P],
                    rhs=x_codes[:, l * T : (l + 1) * T].bitcast(FP8X4),
                    rhs_scale=x_scales[:, l * T : (l + 1) * T],
                    start=True,
                    stop=True,
                )
            enc_bank[n] = bank

        def add_benc(n):
            l, g = enc_chunks[n]
            if g == 0:
                biased[l] = act_pool.tile([P, G, T, PACK], BF16, name="biased", tag="biased")
            nc.vector.tensor_tensor(
                out=biased[l][:, g, :, :],
                in0=enc_bank[n][:].rearrange("p s n -> p n s"),
                in1=benc[:, n - 1 : n, :].to_broadcast([P, T, PACK]),
                op=ADD,
            )

        def relu_layer(l):
            acts[l] = act_pool.tile([P, G * T * PACK], BF16, name="acts", tag="acts", align_bytes=64)
            nc.vector.tensor_scalar_max(
                out=acts[l][:], in0=biased[l][:].rearrange("p g n s -> p (g n s)"), scalar1=0.0
            )

        def quantize_acts(l):
            codes = keep.tile([P, G * T], U32, name="a_codes%d" % l, align_bytes=64)
            scales = keep.tile([P, G * T], U8, name="a_scales%d" % l, align_bytes=64)
            for lo, hi in ((0, 2 * T), (2 * T, 3 * T)):
                nc.vector.quantize_mx(
                    out=codes[:, lo:hi].bitcast(FP8X4),
                    scales=scales[:, lo:hi],
                    in_=acts[l][:, lo * PACK : hi * PACK],
                )
            act_codes[l] = (codes, scales)

        def interleave_columns(engine_copy, grouped, h, raw, lo, hi):
            engine_copy(
                out=grouped[:, h, lo:hi, :].rearrange("p (c i) t -> p c t i", i=RUN),
                in_=raw[:, :, lo:hi].rearrange("p t (c i) -> p c t i", i=RUN),
            )

        def interleave_pair(r):
            grouped = grouped_pool.tile(
                [P, 2, D, PACK], BF16, name="dec_grouped", tag="dec_grouped", align_bytes=64
            )
            dec_grouped[r] = grouped
            for h in range(2):
                raw = dec_raw[2 * r + h]
                split = SCALAR_COLUMNS[r][h]
                if split > 0:
                    interleave_columns(nc.scalar.copy, grouped, h, raw, 0, split)
                if split < D:
                    interleave_columns(nc.vector.tensor_copy, grouped, h, raw, split, D)

        def quantize_pair(r, pieces):
            if r not in dec_codes:
                codes = code_pool.tile([P, 2 * D], U32, name="d_codes", tag="d_codes", align_bytes=64)
                scales = code_pool.tile(
                    [P, 2 * D], U8, name="d_scales", tag="d_scales", align_bytes=64
                )
                dec_codes[r] = (codes, scales)
            codes, scales = dec_codes[r]
            grouped = dec_grouped[r][:].rearrange("p h d t -> p (h d t)")
            for lo, hi in pieces:
                nc.vector.quantize_mx(
                    out=codes[:, lo:hi].bitcast(FP8X4),
                    scales=scales[:, lo:hi],
                    in_=grouped[:, lo * PACK : hi * PACK],
                )

        def decode_pair(r):
            closed = []
            codes, scales = dec_codes[r]
            for h in range(2):
                i, j, g = dec_chunks[2 * r + h]
                first = i == 0 and g == 0
                final = i == j and g == G - 1
                parts = ((0, D),) if j < L - 1 else ((HALF, D), (0, HALF))
                a_codes, a_scales = act_codes[i]
                for lo, hi in parts:
                    if first:
                        acc[(j, lo)] = acc_pool.tile([P, hi - lo], F32, name="acc%d_%d" % (j, lo))
                    nc.tensor.matmul_mx(
                        out=acc[(j, lo)][:],
                        lhsT=a_codes[:, g * T : (g + 1) * T].bitcast(FP8X4),
                        lhsT_scale=a_scales[:, g * T : (g + 1) * T],
                        rhs=codes[:, h * D + lo : h * D + hi].bitcast(FP8X4),
                        rhs_scale=scales[:, h * D + lo : h * D + hi],
                        start=first,
                        stop=final,
                    )
                    if final:
                        closed.append((j, lo, hi))
            return closed

        def add_bdec_and_store(j, lo, hi):
            if j not in staged:
                staged[j] = out_pool.tile([P, D], F32, name="staged", tag="staged")
            nc.vector.tensor_tensor(
                out=staged[j][:, lo:hi],
                in0=acc[(j, lo)][:],
                in1=bdec[:, j * D + lo : j * D + hi],
                op=ADD,
            )
            if lo == 0:
                nc.sync.dma_start(out=out[j], in_=staged[j][:])

        benc_turned = bank_pool.tile([P, 2, P], F32, name="benc_turned", tag="bank")
        for r in range(LOOKAHEAD):
            load_for_round(r)
        transpose_chunk(0)

        next_pair = 0
        outputs_due = {}
        for r in range(n_pairs + 1):
            load_for_round(r + LOOKAHEAD)
            n = r - 1
            finished = layer_finished_in.get(r)
            if r < n_enc:
                empty_transposes(r)
            if 0 <= n < n_enc:
                quantize_chunk(n)
            if 1 <= n < n_enc:
                encode_chunk(n)
            if r + 1 < n_enc:
                transpose_chunk(r + 1)
            if r == 1:
                for u in range(2):
                    nc.tensor.transpose(
                        benc_turned[:, u, :], every_2nd_word(benc_rows[:], u), ident[:]
                    )
            if finished is not None:
                relu_layer(finished)
            if r < n_pairs:
                interleave_pair(r)
            if 1 <= r < n_pairs:
                quantize_pair(r - 1, ((0, 2 * D),))
            if r == n_pairs:
                quantize_pair(r - 1, ((0, D),))
            if r == 1:
                nc.vector.tensor_copy(
                    out=benc[:].bitcast(F32),
                    in_=benc_turned[:, :, 0 : L * G].rearrange("p u c -> p c u"),
                )
            if finished is not None:
                quantize_acts(finished)
            if r == n_pairs:
                quantize_pair(r - 1, ((D + HALF, 2 * D), (D, D + HALF)))
            written = 0
            while (
                written < MAX_PAIRS_A_ROUND
                and next_pair < r
                and all(dec_chunks[2 * next_pair + h][0] in act_codes for h in range(2))
            ):
                for group in decode_pair(next_pair):
                    when = r if r == n_pairs else max(r + 1, FIRST_OUTPUT_ROUND)
                    outputs_due.setdefault(when, []).append(group)
                next_pair += 1
                written += 1
            if 1 <= n < n_enc:
                add_benc(n)
            for j, lo, hi in outputs_due.get(r, []):
                add_bdec_and_store(j, lo, hi)
